import numpy as np
import ml_dtypes

BF16 = ml_dtypes.bfloat16


def bf(x):
    return np.asarray(x, np.float32).astype(BF16)


def f32(x):
    return np.asarray(x, np.float32)


def f64(x):
    return np.asarray(x).astype(np.float64)


def striped(idx):
    return np.tile(idx.reshape(-1, 16).T, (8, 1))


K, S, N, Q, M, A, SB = 128, 512, 512, 4, 512, 128, 256


def setup_inputs():
    return {"table": bf(np.random.standard_normal((K, S))), "w": bf(np.random.standard_normal((K, Q * M)) / np.sqrt(SB)), "offs": striped(np.random.permutation(S)[:N])}


def reference(table, w, offs):
    idx = offs[:16].T.reshape(-1)
    t = f64(table)
    ww = f64(w)
    res = np.zeros((M, A), np.float64)
    for q in range(Q):
        res = res + ww[:, q * M:(q + 1) * M].T @ t[:, idx[q * A:(q + 1) * A]]
    return res

@@ -1,0 +1,42 @@
+import concourse.mybir as mybir
+
+BF16, F32, U16 = mybir.dt.bfloat16, mybir.dt.float32, mybir.dt.uint16
+
+P = 128
+S = 512
+Q = 4
+A = 128
+M = 512
+ROW_BLOCKS = M // P
+LIST_COLUMNS = A // 16
+
+FLOPS = 2 * M * A * Q * P
+
+
+def tile_h_kernel(tc, table, w, offs, out):
+    nc = tc.nc
+    with (
+        tc.tile_pool(name="held", bufs=1) as held,
+        tc.psum_pool(name="psum", bufs=1) as psum,
+    ):
+        offsets = held.tile([P, Q * LIST_COLUMNS], U16, name="offsets")
+        nc.sync.dma_start(offsets[:], offs)
+        signal = held.tile([P, S], BF16, name="signal")
+        nc.sync.dma_start(signal[:], table)
+        weights = held.tile([P, Q * M], BF16, name="weights")
+        nc.scalar.dma_start(weights[:], w)
+
+        staged = held.tile([P, ROW_BLOCKS, A], F32, name="staged")
+        for b in range(ROW_BLOCKS):
+            acc = psum.tile([P, A], F32, name=f"acc{b}")
+            for q in range(Q):
+                picked = signal[:].indirect(offsets[:, q * LIST_COLUMNS : (q + 1) * LIST_COLUMNS])
+                nc.tensor.matmul(
+                    acc[:],
+                    weights[:, q * M + b * P : q * M + (b + 1) * P],
+                    picked,
+                    start=(q == 0),
+                    stop=(q == Q - 1),
+                )
+            nc.vector.tensor_copy(staged[:, b, :], acc[:])
+        nc.sync.dma_start(out.rearrange("(b p) a -> p b a", p=P), staged[:])

@@ -22,21 +22,30 @@ def tile_h_kernel(tc, table, w, offs, out):
         offsets = held.tile([P, Q * LIST_COLUMNS], U16, name="offsets")
         nc.sync.dma_start(offsets[:], offs)
         signal = held.tile([P, S], BF16, name="signal")
-        nc.sync.dma_start(signal[:], table)
-        weights = held.tile([P, Q * M], BF16, name="weights")
-        nc.scalar.dma_start(weights[:], w)
+        nc.scalar.dma_start(signal[:], table)
+        queues = [nc.sync, nc.scalar]
+        weights = []
+        for q in range(Q):
+            slot_weights = held.tile([P, M], BF16, name=f"weights{q}")
+            queues[q % 2].dma_start(slot_weights[:], w[:, q * M : (q + 1) * M])
+            weights.append(slot_weights)
 
-        staged = held.tile([P, ROW_BLOCKS, A], F32, name="staged")
-        for b in range(ROW_BLOCKS):
-            acc = psum.tile([P, A], F32, name=f"acc{b}")
-            for q in range(Q):
-                picked = signal[:].indirect(offsets[:, q * LIST_COLUMNS : (q + 1) * LIST_COLUMNS])
+        accs = [psum.tile([P, A], F32, name=f"acc{b}") for b in range(ROW_BLOCKS)]
+        for q in range(Q):
+            picked = signal[:].indirect(offsets[:, q * LIST_COLUMNS : (q + 1) * LIST_COLUMNS])
+            for b in range(ROW_BLOCKS):
                 nc.tensor.matmul(
-                    acc[:],
-                    weights[:, q * M + b * P : q * M + (b + 1) * P],
+                    accs[b][:],
+                    weights[q][:, b * P : (b + 1) * P],
                     picked,
                     start=(q == 0),
                     stop=(q == Q - 1),
                 )
-            nc.vector.tensor_copy(staged[:, b, :], acc[:])
-        nc.sync.dma_start(out.rearrange("(b p) a -> p b a", p=P), staged[:])
+
+        for b in range(ROW_BLOCKS):
+            staged = held.tile([P, A], F32, name=f"staged{b}")
+            if b % 2 == 0:
+                nc.vector.tensor_copy(staged[:], accs[b][:])
+            else:
+                nc.scalar.copy(staged[:], accs[b][:])
+            queues[b % 2].dma_start(out[b * P : (b + 1) * P, :], staged[:])

@@ -12,6 +12,9 @@ LIST_COLUMNS = A // 16
 
 FLOPS = 2 * M * A * Q * P
 
+WARM_COLUMNS = 512
+WARM_MATMULS = 6
+
 
 def tile_h_kernel(tc, table, w, offs, out):
     nc = tc.nc
@@ -29,6 +32,12 @@ def tile_h_kernel(tc, table, w, offs, out):
             slot_weights = held.tile([P, M], BF16, name=f"weights{q}")
             queues[q % 2].dma_start(slot_weights[:], w[:, q * M : (q + 1) * M])
             weights.append(slot_weights)
+
+        zeros = held.tile([P, WARM_COLUMNS], BF16, name="zeros")
+        nc.vector.memset(zeros[:], 0.0)
+        unread = psum.tile([P, WARM_COLUMNS], F32, name="unread")
+        for repeat in range(WARM_MATMULS):
+            nc.tensor.matmul(unread[:], zeros[:, 0:P], zeros[:], start=True, stop=True)
 
         accs = [psum.tile([P, A], F32, name=f"acc{b}") for b in range(ROW_BLOCKS)]
         for q in range(Q):

@@ -12,9 +12,6 @@ LIST_COLUMNS = A // 16
 
 FLOPS = 2 * M * A * Q * P
 
-WARM_COLUMNS = 512
-WARM_MATMULS = 6
-
 
 def tile_h_kernel(tc, table, w, offs, out):
     nc = tc.nc
@@ -26,35 +23,19 @@ def tile_h_kernel(tc, table, w, offs, out):
         nc.sync.dma_start(offsets[:], offs)
         signal = held.tile([P, S], BF16, name="signal")
         nc.scalar.dma_start(signal[:], table)
+        w_by_block = w.rearrange("k (q b m) -> b k q m", q=Q, b=ROW_BLOCKS)
         queues = [nc.sync, nc.scalar]
         weights = []
-        for q in range(Q):
-            slot_weights = held.tile([P, M], BF16, name=f"weights{q}")
-            queues[q % 2].dma_start(slot_weights[:], w[:, q * M : (q + 1) * M])
-            weights.append(slot_weights)
-
-        zeros = held.tile([P, WARM_COLUMNS], BF16, name="zeros")
-        nc.vector.memset(zeros[:], 0.0)
-        unread = psum.tile([P, WARM_COLUMNS], F32, name="unread")
-        for repeat in range(WARM_MATMULS):
-            nc.tensor.matmul(unread[:], zeros[:, 0:P], zeros[:], start=True, stop=True)
-
-        accs = [psum.tile([P, A], F32, name=f"acc{b}") for b in range(ROW_BLOCKS)]
-        for q in range(Q):
-            picked = signal[:].indirect(offsets[:, q * LIST_COLUMNS : (q + 1) * LIST_COLUMNS])
-            for b in range(ROW_BLOCKS):
-                nc.tensor.matmul(
-                    accs[b][:],
-                    weights[q][:, b * P : (b + 1) * P],
-                    picked,
-                    start=(q == 0),
-                    stop=(q == Q - 1),
-                )
+        for b in range(ROW_BLOCKS):
+            block_weights = held.tile([P, Q, P], BF16, name=f"weights{b}")
+            queues[b % 2].dma_start(block_weights[:], w_by_block[b])
+            weights.append(block_weights)
 
         for b in range(ROW_BLOCKS):
+            acc = psum.tile([P, A], F32, name=f"acc{b}")
+            for q in range(Q):
+                picked = signal[:].indirect(offsets[:, q * LIST_COLUMNS : (q + 1) * LIST_COLUMNS])
+                nc.tensor.matmul(acc[:], weights[b][:, q, :], picked, start=(q == 0), stop=(q == Q - 1))
             staged = held.tile([P, A], F32, name=f"staged{b}")
-            if b % 2 == 0:
-                nc.vector.tensor_copy(staged[:], accs[b][:])
-            else:
-                nc.scalar.copy(staged[:], accs[b][:])
-            queues[b % 2].dma_start(out[b * P : (b + 1) * P, :], staged[:])
+            nc.vector.tensor_copy(staged[:], acc[:])
+            nc.sync.dma_start(out[b * P : (b + 1) * P, :], staged[:])

@@ -23,19 +23,25 @@ def tile_h_kernel(tc, table, w, offs, out):
         nc.sync.dma_start(offsets[:], offs)
         signal = held.tile([P, S], BF16, name="signal")
         nc.scalar.dma_start(signal[:], table)
-        w_by_block = w.rearrange("k (q b m) -> b k q m", q=Q, b=ROW_BLOCKS)
-        queues = [nc.sync, nc.scalar]
-        weights = []
-        for b in range(ROW_BLOCKS):
-            block_weights = held.tile([P, Q, P], BF16, name=f"weights{b}")
-            queues[b % 2].dma_start(block_weights[:], w_by_block[b])
-            weights.append(block_weights)
+        first_weights = held.tile([P, M], BF16, name="first_weights")
+        nc.sync.dma_start(first_weights[:], w[:, 0:M])
+        later_weights = held.tile([P, (Q - 1) * M], BF16, name="later_weights")
+        nc.scalar.dma_start(later_weights[:], w[:, M : Q * M])
 
+        def project(acc, b, q):
+            picked = signal[:].indirect(offsets[:, q * LIST_COLUMNS : (q + 1) * LIST_COLUMNS])
+            if q == 0:
+                block_weights = first_weights[:, b * P : (b + 1) * P]
+            else:
+                block_weights = later_weights[:, (q - 1) * M + b * P : (q - 1) * M + (b + 1) * P]
+            nc.tensor.matmul(acc[:], block_weights, picked, start=(q == 0), stop=(q == Q - 1))
+
+        accs = [psum.tile([P, A], F32, name=f"acc{b}") for b in range(ROW_BLOCKS)]
         for b in range(ROW_BLOCKS):
-            acc = psum.tile([P, A], F32, name=f"acc{b}")
-            for q in range(Q):
-                picked = signal[:].indirect(offsets[:, q * LIST_COLUMNS : (q + 1) * LIST_COLUMNS])
-                nc.tensor.matmul(acc[:], weights[b][:, q, :], picked, start=(q == 0), stop=(q == Q - 1))
+            project(accs[b], b, 0)
+        for b in range(ROW_BLOCKS):
+            for q in range(1, Q):
+                project(accs[b], b, q)
             staged = held.tile([P, A], F32, name=f"staged{b}")
-            nc.vector.tensor_copy(staged[:], acc[:])
+            nc.vector.tensor_copy(staged[:], accs[b][:])
             nc.sync.dma_start(out[b * P : (b + 1) * P, :], staged[:])

@@ -12,6 +12,8 @@ LIST_COLUMNS = A // 16
 
 FLOPS = 2 * M * A * Q * P
 
+PIECES = [(0, M), (M, 2 * M), (2 * M, 4 * M)]
+
 
 def tile_h_kernel(tc, table, w, offs, out):
     nc = tc.nc
@@ -20,28 +22,37 @@ def tile_h_kernel(tc, table, w, offs, out):
         tc.psum_pool(name="psum", bufs=1) as psum,
     ):
         offsets = held.tile([P, Q * LIST_COLUMNS], U16, name="offsets")
-        nc.sync.dma_start(offsets[:], offs)
         signal = held.tile([P, S], BF16, name="signal")
+        nc.sync.dma_start(offsets[:], offs)
         nc.scalar.dma_start(signal[:], table)
-        first_weights = held.tile([P, M], BF16, name="first_weights")
-        nc.sync.dma_start(first_weights[:], w[:, 0:M])
-        later_weights = held.tile([P, (Q - 1) * M], BF16, name="later_weights")
-        nc.scalar.dma_start(later_weights[:], w[:, M : Q * M])
+        pieces = []
+        for i, (first, end) in enumerate(PIECES):
+            piece = held.tile([P, end - first], BF16, name=f"weights{i}")
+            (nc.sync if i == 0 else nc.scalar).dma_start(piece[:], w[:, first:end])
+            pieces.append(piece)
+
+        def block_weights(b, q):
+            column = q * M + b * P
+            for piece, (first, end) in zip(pieces, PIECES):
+                if first <= column < end:
+                    return piece[:, column - first : column - first + P]
 
         def project(acc, b, q):
             picked = signal[:].indirect(offsets[:, q * LIST_COLUMNS : (q + 1) * LIST_COLUMNS])
-            if q == 0:
-                block_weights = first_weights[:, b * P : (b + 1) * P]
-            else:
-                block_weights = later_weights[:, (q - 1) * M + b * P : (q - 1) * M + (b + 1) * P]
-            nc.tensor.matmul(acc[:], block_weights, picked, start=(q == 0), stop=(q == Q - 1))
+            nc.tensor.matmul(acc[:], block_weights(b, q), picked, start=(q == 0), stop=(q == Q - 1))
 
         accs = [psum.tile([P, A], F32, name=f"acc{b}") for b in range(ROW_BLOCKS)]
         for b in range(ROW_BLOCKS):
             project(accs[b], b, 0)
+        staged_pair = held.tile([P, 2, A], F32, name="staged_pair")
         for b in range(ROW_BLOCKS):
             for q in range(1, Q):
                 project(accs[b], b, q)
-            staged = held.tile([P, A], F32, name=f"staged{b}")
-            nc.vector.tensor_copy(staged[:], accs[b][:])
-            nc.sync.dma_start(out[b * P : (b + 1) * P, :], staged[:])
+            if b < 2:
+                nc.vector.tensor_copy(staged_pair[:, b, :], accs[b][:])
+            else:
+                staged = held.tile([P, A], F32, name=f"staged{b}")
+                nc.vector.tensor_copy(staged[:], accs[b][:])
+                nc.sync.dma_start(out[b * P : (b + 1) * P, :], staged[:])
+            if b == 1:
+                nc.sync.dma_start(out[0 : 2 * P, :].rearrange("(b p) a -> p b a", p=P), staged_pair[:])

@@ -12,7 +12,7 @@ LIST_COLUMNS = A // 16
 
 FLOPS = 2 * M * A * Q * P
 
-PIECES = [(0, M), (M, 2 * M), (2 * M, 4 * M)]
+PIECES = [(0, 2 * P), (2 * P, 2 * M), (2 * M, 4 * M)]
 
 
 def tile_h_kernel(tc, table, w, offs, out):

@@ -24,11 +24,11 @@ def tile_h_kernel(tc, table, w, offs, out):
         offsets = held.tile([P, Q * LIST_COLUMNS], U16, name="offsets")
         signal = held.tile([P, S], BF16, name="signal")
         nc.sync.dma_start(offsets[:], offs)
-        nc.scalar.dma_start(signal[:], table)
+        nc.sync.dma_start(signal[:], table)
         pieces = []
         for i, (first, end) in enumerate(PIECES):
             piece = held.tile([P, end - first], BF16, name=f"weights{i}")
-            (nc.sync if i == 0 else nc.scalar).dma_start(piece[:], w[:, first:end])
+            nc.scalar.dma_start(piece[:], w[:, first:end])
             pieces.append(piece)
 
         def block_weights(b, q):

@@ -12,7 +12,7 @@ LIST_COLUMNS = A // 16
 
 FLOPS = 2 * M * A * Q * P
 
-PIECES = [(0, 2 * P), (2 * P, 2 * M), (2 * M, 4 * M)]
+PIECES = [(0, 3 * P), (3 * P, 8 * P), (8 * P, 16 * P)]
 
 
 def tile_h_kernel(tc, table, w, offs, out):

@@ -23,8 +23,8 @@ def tile_h_kernel(tc, table, w, offs, out):
     ):
         offsets = held.tile([P, Q * LIST_COLUMNS], U16, name="offsets")
         signal = held.tile([P, S], BF16, name="signal")
-        nc.sync.dma_start(offsets[:], offs)
         nc.sync.dma_start(signal[:], table)
+        nc.sync.dma_start(offsets[:], offs)
         pieces = []
         for i, (first, end) in enumerate(PIECES):
             piece = held.tile([P, end - first], BF16, name=f"weights{i}")

import concourse.mybir as mybir

BF16, F32, U16 = mybir.dt.bfloat16, mybir.dt.float32, mybir.dt.uint16

P = 128
S = 512
Q = 4
A = 128
M = 512
ROW_BLOCKS = M // P
LIST_COLUMNS = A // 16

FLOPS = 2 * M * A * Q * P

PIECES = [(0, 3 * P), (3 * P, 8 * P), (8 * P, 16 * P)]


def tile_h_kernel(tc, table, w, offs, out):
    nc = tc.nc
    with (
        tc.tile_pool(name="held", bufs=1) as held,
        tc.psum_pool(name="psum", bufs=1) as psum,
    ):
        offsets = held.tile([P, Q * LIST_COLUMNS], U16, name="offsets")
        signal = held.tile([P, S], BF16, name="signal")
        nc.sync.dma_start(signal[:], table)
        nc.sync.dma_start(offsets[:], offs)
        pieces = []
        for i, (first, end) in enumerate(PIECES):
            piece = held.tile([P, end - first], BF16, name=f"weights{i}")
            nc.scalar.dma_start(piece[:], w[:, first:end])
            pieces.append(piece)

        def block_weights(b, q):
            column = q * M + b * P
            for piece, (first, end) in zip(pieces, PIECES):
                if first <= column < end:
                    return piece[:, column - first : column - first + P]

        def project(acc, b, q):
            picked = signal[:].indirect(offsets[:, q * LIST_COLUMNS : (q + 1) * LIST_COLUMNS])
            nc.tensor.matmul(acc[:], block_weights(b, q), picked, start=(q == 0), stop=(q == Q - 1))

        accs = [psum.tile([P, A], F32, name=f"acc{b}") for b in range(ROW_BLOCKS)]
        for b in range(ROW_BLOCKS):
            project(accs[b], b, 0)
        staged_pair = held.tile([P, 2, A], F32, name="staged_pair")
        for b in range(ROW_BLOCKS):
            for q in range(1, Q):
                project(accs[b], b, q)
            if b < 2:
                nc.vector.tensor_copy(staged_pair[:, b, :], accs[b][:])
            else:
                staged = held.tile([P, A], F32, name=f"staged{b}")
                nc.vector.tensor_copy(staged[:], accs[b][:])
                nc.sync.dma_start(out[b * P : (b + 1) * P, :], staged[:])
            if b == 1:
                nc.sync.dma_start(out[0 : 2 * P, :].rearrange("(b p) a -> p b a", p=P), staged_pair[:])
